import numpy as np
import ml_dtypes


def mxq(x, axis, fmt="e4m3"):
    dtype, down = {"e4m3": (ml_dtypes.float8_e4m3fn, 7), "e5m2": (ml_dtypes.float8_e5m2, 14)}[fmt]
    v = np.moveaxis(np.asarray(x, np.float32).astype(ml_dtypes.bfloat16).astype(np.float64), axis, -1)
    blocks = v.reshape(v.shape[:-1] + (-1, 32))
    amax = np.abs(blocks).max(-1, keepdims=True)
    byte = np.maximum(np.where(amax > 0, np.frexp(amax)[1] - 1 + 127, 0) - down, 1)
    scale = np.exp2(byte - 127.0)
    codes = (blocks / scale).astype(np.float32).astype(dtype).astype(np.float64)
    return np.moveaxis((codes * scale).reshape(v.shape), -1, axis)


WIDE = False


def mx_kscale(k):
    if not WIDE:
        return np.ones(k)
    levels = np.array([10, -10, 5, -5, 0])
    a = np.random.permutation(np.resize(levels, k // 512 * 4)).reshape(k // 512, 4)
    idx = np.arange(k)
    return np.exp2(a[idx // 512, idx % 128 // 32])


BF16 = ml_dtypes.bfloat16


def bf(x):
    return np.asarray(x, np.float32).astype(BF16)


def f64(x):
    return np.asarray(x).astype(np.float64)


B, T, HS, C, NH, HD, WS, MAXD = 2, 8, 28, 512, 8, 16, 7, 3
N = T * HS * HS
E = NH * HD
BT = B * NH * T
EPS = 1e-12


def l2norm(v, axis):
    return v / np.maximum(np.sqrt(np.sum(v * v, axis=axis, keepdims=True)), EPS)


def setup_inputs():
    s = mx_kscale(C)
    return {"x": bf(np.random.standard_normal((B, N, C)) * s),
            "q_w": bf(np.random.standard_normal((E, C)) / np.sqrt(C) / s),
            "k_w": bf(np.random.standard_normal((E, C)) / np.sqrt(C) / s)}


def reference(x, q_w, k_w):
    xq = mxq(f64(x), 2, "e4m3")
    q = xq @ mxq(f64(q_w), 1, "e4m3").T
    k = xq @ mxq(f64(k_w), 1, "e4m3").T
    q = q.reshape(B, N, NH, HD).transpose(0, 2, 1, 3)
    k = k.reshape(B, N, NH, HD).transpose(0, 2, 1, 3)
    q = q.reshape(B * NH, T, HS, HS, HD).transpose(0, 1, 4, 2, 3)
    k = k.reshape(B * NH, T, HS, HS, HD).transpose(0, 1, 4, 2, 3)
    k_post = np.concatenate([k[:, 1:], k[:, -1:]], axis=1)
    qp = l2norm(q.reshape(BT, HD, HS, HS), 1)
    kp = l2norm(k_post.reshape(BT, HD, HS, HS), 1)
    return qp, kp

@@ -1,0 +1,203 @@
+from contextlib import ExitStack
+
+import concourse.mybir as mybir
+from concourse.masks import make_identity
+
+F32 = mybir.dt.float32
+BF16 = mybir.dt.bfloat16
+U32 = mybir.dt.uint32
+U8 = mybir.dt.uint8
+FP8X4 = mybir.dt.float8_e4m3fn_x4
+ACT = mybir.ActivationFunctionType
+ALU = mybir.AluOpType
+
+P = 128
+CLIPS, FRAMES_PER_CLIP, FRAME = 2, 8, 28 * 28
+FRAMES = CLIPS * FRAMES_PER_CLIP
+TOKENS = FRAMES * FRAME
+CHANNELS = 512
+PACK = 4
+HALVES = 2
+KINDS = 2
+HEADS, HEAD_DIM = 8, 16
+ROWS = 2
+BLOCK = ROWS * P
+BLOCKS = TOKENS // BLOCK
+GROUPS = ROWS * KINDS * HEADS
+EPS = 1e-12
+
+LOADS_AHEAD = 4
+LAG_REGROUP = 1
+LAG_QUANTISE = 2
+LAG_MULTIPLY = 3
+LAG_SUM = 4
+LAG_INVERT = 5
+LAG_NORMALISE = 6
+LAG_TRANSPOSE_BACK = 7
+LAG_STAGE = 8
+LAG_STORE = 9
+STAGE_ON_VECTOR_EVERY = 4
+
+FLOPS = 2 * TOKENS * CHANNELS * KINDS * HEADS * HEAD_DIM
+
+
+def tile_costvolumeattention17_pa_t_kernel(tc, x, q_w, k_w, out_0, out_1):
+    nc = tc.nc
+    assert TOKENS == BLOCKS * BLOCK
+
+    x_blocks = x.flatten_outer_dims().rearrange("(c p r) k -> c p (r k)", p=P, r=ROWS)
+    q_frames = out_0.rearrange("(b h t) d i j -> b t d h (i j)", b=CLIPS, h=HEADS)
+    k_frames = out_1.rearrange("(b h t) d i j -> b t d h (i j)", b=CLIPS, h=HEADS)
+
+    with ExitStack() as ctx:
+        ctx.enter_context(tc.manual_schedule())
+        keep = ctx.enter_context(tc.tile_pool(name="keep", bufs=1))
+        loads = ctx.enter_context(tc.tile_pool(name="loads", bufs=LOADS_AHEAD + 2))
+        work = ctx.enter_context(tc.tile_pool(name="work", bufs=3))
+        psum_in = ctx.enter_context(tc.psum_pool(name="psum_in", bufs=2))
+        psum_mx = ctx.enter_context(tc.psum_pool(name="psum_mx", bufs=4))
+        psum_out = ctx.enter_context(tc.psum_pool(name="psum_out", bufs=2))
+
+        identity = keep.tile([P, P], F32)
+        make_identity(nc, identity[:])
+        staged = keep.tile([P, KINDS, TOKENS], F32)
+
+        def transpose_words(rows):
+            words = rows.bitcast(F32)
+            flipped = psum_in.tile([P, ROWS, HALVES, P], F32)
+            for r in range(ROWS):
+                for u in range(HALVES):
+                    first = (r * HALVES + u) * P
+                    nc.tensor.transpose(flipped[:, r, u, :], words[:, first : first + P], identity[:])
+            return flipped
+
+        def regroup(flipped):
+            grouped = work.tile([P, BLOCK * PACK], BF16, align_bytes=64)
+            nc.scalar.copy(
+                out=grouped[:].bitcast(F32).rearrange("q (r m u) -> q r m u", r=ROWS, u=HALVES),
+                in_=flipped[:].rearrange("q r u m -> q r m u"),
+            )
+            return grouped
+
+        def quantise(grouped, codes, scales):
+            nc.vector.quantize_mx(out=codes[:].bitcast(FP8X4), scales=scales[:], in_=grouped[:])
+
+        x_rows, x_flipped, x_grouped, x_codes, x_scales = {}, {}, {}, {}, {}
+        products, squares, sums, inverse_norms, normalised, out_flipped = {}, {}, {}, {}, {}, {}
+
+        def load(c):
+            x_rows[c] = loads.tile([P, ROWS * CHANNELS], BF16, name="x_rows")
+            nc.sync.dma_start(out=x_rows[c][:], in_=x_blocks[c])
+
+        def transpose_in(c):
+            x_flipped[c] = transpose_words(x_rows[c][:])
+
+        def regroup_block(c):
+            x_grouped[c] = regroup(x_flipped[c])
+
+        def quantise_block(c):
+            x_codes[c] = work.tile([P, BLOCK], U32, name="x_codes", align_bytes=64)
+            x_scales[c] = work.tile([P, BLOCK], U8, name="x_scales", align_bytes=64)
+            quantise(x_grouped[c], x_codes[c], x_scales[c])
+
+        def multiply(c):
+            products[c] = psum_mx.tile([P, ROWS, KINDS * P], F32, name="products")
+            for r in range(ROWS):
+                tokens = slice(r * P, (r + 1) * P)
+                nc.tensor.matmul_mx(
+                    out=products[c][:, r, :],
+                    lhsT=x_codes[c][:, tokens].bitcast(FP8X4),
+                    lhsT_scale=x_scales[c][:, tokens],
+                    rhs=w_codes[:].bitcast(FP8X4),
+                    rhs_scale=w_scales[:],
+                    start=True,
+                    stop=True,
+                )
+
+        def square(c):
+            squares[c] = work.tile([P, GROUPS, HEAD_DIM], F32, name="squares")
+            nc.scalar.activation(
+                out=squares[c][:].rearrange("p g d -> p (g d)"),
+                in_=products[c][:].rearrange("p r e -> p (r e)"),
+                func=ACT.Square,
+            )
+
+        def sum_squares(c):
+            sums[c] = work.tile([P, GROUPS], F32, name="sums")
+            nc.vector.tensor_reduce(out=sums[c][:], in_=squares[c][:], axis=mybir.AxisListType.X, op=ALU.add)
+
+        def clamp(c):
+            nc.vector.tensor_scalar_max(out=sums[c][:], in0=sums[c][:], scalar1=EPS * EPS)
+
+        def invert(c):
+            inverse_norms[c] = work.tile([P, GROUPS], F32, name="inverse_norms")
+            nc.scalar.activation(out=inverse_norms[c][:], in_=sums[c][:], func=ACT.Abs_reciprocal_sqrt)
+
+        def normalise(c):
+            normalised[c] = work.tile([P, ROWS * KINDS, HEAD_DIM, HEADS], F32, name="normalised")
+            nc.vector.tensor_tensor(
+                out=normalised[c][:],
+                in0=products[c][:].rearrange("p r (k h d) -> p (r k) d h", k=KINDS, h=HEADS),
+                in1=inverse_norms[c][:]
+                .rearrange("p (a h) -> p a h", h=HEADS)
+                .unsqueeze(2)
+                .to_broadcast([P, ROWS * KINDS, HEAD_DIM, HEADS]),
+                op=ALU.mult,
+            )
+
+        def transpose_back(c):
+            out_flipped[c] = psum_out.tile([P, KINDS, ROWS, P], F32, name="out_flipped")
+            for r in range(ROWS):
+                for k in range(KINDS):
+                    nc.tensor.transpose(
+                        out_flipped[c][:, k, r, :],
+                        normalised[c][:, r * KINDS + k, :, :].rearrange("p d h -> p (d h)"),
+                        identity[:],
+                    )
+
+        def stage(c):
+            target = staged[:, :, c * BLOCK : (c + 1) * BLOCK].rearrange("e k (m r) -> e k m r", r=ROWS)
+            source = out_flipped[c][:].rearrange("e k r m -> e k m r")
+            if c % STAGE_ON_VECTOR_EVERY == 0:
+                nc.vector.tensor_copy(out=target, in_=source)
+            else:
+                nc.scalar.copy(out=target, in_=source)
+
+        def store_frames_finished_by(c):
+            for f in range(FRAMES):
+                if c * BLOCK < (f + 1) * FRAME <= (c + 1) * BLOCK:
+                    b, t = divmod(f, FRAMES_PER_CLIP)
+                    tokens = slice(f * FRAME, (f + 1) * FRAME)
+                    nc.sync.dma_start(out=q_frames[b, t], in_=staged[:, 0, tokens])
+                    if t > 0:
+                        nc.sync.dma_start(out=k_frames[b, t - 1], in_=staged[:, 1, tokens])
+                    if t == FRAMES_PER_CLIP - 1:
+                        nc.sync.dma_start(out=k_frames[b, t], in_=staged[:, 1, tokens])
+
+        w_rows = keep.tile([P, KINDS * CHANNELS], BF16)
+        nc.scalar.dma_start(out=w_rows[:, 0:CHANNELS], in_=q_w)
+        nc.scalar.dma_start(out=w_rows[:, CHANNELS : KINDS * CHANNELS], in_=k_w)
+        for c in range(LOADS_AHEAD):
+            load(c)
+        w_codes = keep.tile([P, KINDS * P], U32, align_bytes=64)
+        w_scales = keep.tile([P, KINDS * P], U8, align_bytes=64)
+        quantise(regroup(transpose_words(w_rows[:])), w_codes, w_scales)
+
+        def run(step, c):
+            if 0 <= c < BLOCKS:
+                step(c)
+
+        for n in range(BLOCKS + LAG_STORE):
+            run(load, n + LOADS_AHEAD)
+            run(store_frames_finished_by, n - LAG_STORE)
+            run(quantise_block, n - LAG_QUANTISE)
+            run(multiply, n - LAG_MULTIPLY)
+            run(transpose_in, n)
+            run(transpose_back, n - LAG_TRANSPOSE_BACK)
+            run(regroup_block, n - LAG_REGROUP)
+            run(clamp, n - LAG_INVERT)
+            run(normalise, n - LAG_NORMALISE)
+            run(stage, n - LAG_STAGE)
+            run(sum_squares, n - LAG_SUM)
+            run(invert, n - LAG_INVERT)
+            run(square, n - LAG_MULTIPLY)

@@ -26,7 +26,7 @@ BLOCKS = TOKENS // BLOCK
 GROUPS = ROWS * KINDS * HEADS
 EPS = 1e-12
 
-LOADS_AHEAD = 4
+LOADS_AHEAD = 6
 LAG_REGROUP = 1
 LAG_QUANTISE = 2
 LAG_MULTIPLY = 3
@@ -35,7 +35,6 @@ LAG_INVERT = 5
 LAG_NORMALISE = 6
 LAG_TRANSPOSE_BACK = 7
 LAG_STAGE = 8
-LAG_STORE = 9
 STAGE_ON_VECTOR_EVERY = 4
 
 FLOPS = 2 * TOKENS * CHANNELS * KINDS * HEADS * HEAD_DIM
@@ -54,13 +53,13 @@ def tile_costvolumeattention17_pa_t_kernel(tc, x, q_w, k_w, out_0, out_1):
         keep = ctx.enter_context(tc.tile_pool(name="keep", bufs=1))
         loads = ctx.enter_context(tc.tile_pool(name="loads", bufs=LOADS_AHEAD + 2))
         work = ctx.enter_context(tc.tile_pool(name="work", bufs=3))
+        frames = ctx.enter_context(tc.tile_pool(name="frames", bufs=3))
         psum_in = ctx.enter_context(tc.psum_pool(name="psum_in", bufs=2))
         psum_mx = ctx.enter_context(tc.psum_pool(name="psum_mx", bufs=4))
         psum_out = ctx.enter_context(tc.psum_pool(name="psum_out", bufs=2))
 
         identity = keep.tile([P, P], F32)
         make_identity(nc, identity[:])
-        staged = keep.tile([P, KINDS, TOKENS], F32)
 
         def transpose_words(rows):
             words = rows.bitcast(F32)
@@ -83,7 +82,7 @@ def tile_costvolumeattention17_pa_t_kernel(tc, x, q_w, k_w, out_0, out_1):
             nc.vector.quantize_mx(out=codes[:].bitcast(FP8X4), scales=scales[:], in_=grouped[:])
 
         x_rows, x_flipped, x_grouped, x_codes, x_scales = {}, {}, {}, {}, {}
-        products, squares, sums, inverse_norms, normalised, out_flipped = {}, {}, {}, {}, {}, {}
+        products, squares, sums, inverse_norms, normalised, out_flipped, staged = {}, {}, {}, {}, {}, {}, {}
 
         def load(c):
             x_rows[c] = loads.tile([P, ROWS * CHANNELS], BF16, name="x_rows")
@@ -156,23 +155,30 @@ def tile_costvolumeattention17_pa_t_kernel(tc, x, q_w, k_w, out_0, out_1):
                     )
 
         def stage(c):
-            target = staged[:, :, c * BLOCK : (c + 1) * BLOCK].rearrange("e k (m r) -> e k m r", r=ROWS)
-            source = out_flipped[c][:].rearrange("e k r m -> e k m r")
-            if c % STAGE_ON_VECTOR_EVERY == 0:
-                nc.vector.tensor_copy(out=target, in_=source)
-            else:
-                nc.scalar.copy(out=target, in_=source)
+            copy = nc.vector.tensor_copy if c % STAGE_ON_VECTOR_EVERY == 0 else nc.scalar.copy
+            for f in range(c * BLOCK // FRAME, ((c + 1) * BLOCK - 1) // FRAME + 1):
+                first = max(c * BLOCK, f * FRAME)
+                last = min((c + 1) * BLOCK, (f + 1) * FRAME)
+                if first == f * FRAME:
+                    staged[f] = frames.tile([P, KINDS, FRAME], F32, name="staged")
+                copy(
+                    out=staged[f][:, :, first - f * FRAME : last - f * FRAME].rearrange(
+                        "e k (m r) -> e k m r", r=ROWS
+                    ),
+                    in_=out_flipped[c][:, :, :, (first - c * BLOCK) // ROWS : (last - c * BLOCK) // ROWS].rearrange(
+                        "e k r m -> e k m r"
+                    ),
+                )
+                if last == (f + 1) * FRAME:
+                    store(f)
 
-        def store_frames_finished_by(c):
-            for f in range(FRAMES):
-                if c * BLOCK < (f + 1) * FRAME <= (c + 1) * BLOCK:
-                    b, t = divmod(f, FRAMES_PER_CLIP)
-                    tokens = slice(f * FRAME, (f + 1) * FRAME)
-                    nc.sync.dma_start(out=q_frames[b, t], in_=staged[:, 0, tokens])
-                    if t > 0:
-                        nc.sync.dma_start(out=k_frames[b, t - 1], in_=staged[:, 1, tokens])
-                    if t == FRAMES_PER_CLIP - 1:
-                        nc.sync.dma_start(out=k_frames[b, t], in_=staged[:, 1, tokens])
+        def store(f):
+            b, t = divmod(f, FRAMES_PER_CLIP)
+            nc.sync.dma_start(out=q_frames[b, t], in_=staged[f][:, 0, :])
+            if t > 0:
+                nc.sync.dma_start(out=k_frames[b, t - 1], in_=staged[f][:, 1, :])
+            if t == FRAMES_PER_CLIP - 1:
+                nc.sync.dma_start(out=k_frames[b, t], in_=staged[f][:, 1, :])
 
         w_rows = keep.tile([P, KINDS * CHANNELS], BF16)
         nc.scalar.dma_start(out=w_rows[:, 0:CHANNELS], in_=q_w)
@@ -187,9 +193,8 @@ def tile_costvolumeattention17_pa_t_kernel(tc, x, q_w, k_w, out_0, out_1):
             if 0 <= c < BLOCKS:
                 step(c)
 
-        for n in range(BLOCKS + LAG_STORE):
+        for n in range(BLOCKS + LAG_STAGE):
             run(load, n + LOADS_AHEAD)
-            run(store_frames_finished_by, n - LAG_STORE)
             run(quantise_block, n - LAG_QUANTISE)
             run(multiply, n - LAG_MULTIPLY)
             run(transpose_in, n)

@@ -21,9 +21,8 @@ HALVES = 2
 KINDS = 2
 HEADS, HEAD_DIM = 8, 16
 ROWS = 2
-BLOCK = ROWS * P
-BLOCKS = TOKENS // BLOCK
-GROUPS = ROWS * KINDS * HEADS
+CHUNK = ROWS * P
+CHUNKS = TOKENS // CHUNK
 EPS = 1e-12
 
 LOADS_AHEAD = 6
@@ -40,11 +39,23 @@ STAGE_ON_VECTOR_EVERY = 4
 FLOPS = 2 * TOKENS * CHANNELS * KINDS * HEADS * HEAD_DIM
 
 
+def frames_of(c):
+    return range(c * CHUNK // FRAME, ((c + 1) * CHUNK - 1) // FRAME + 1)
+
+
+def kinds_of_frame(f):
+    return 1 if f % FRAMES_PER_CLIP == 0 else KINDS
+
+
+def kinds_of(c):
+    return max(kinds_of_frame(f) for f in frames_of(c))
+
+
 def tile_costvolumeattention17_pa_t_kernel(tc, x, q_w, k_w, out_0, out_1):
     nc = tc.nc
-    assert TOKENS == BLOCKS * BLOCK
+    assert TOKENS == CHUNKS * CHUNK
 
-    x_blocks = x.flatten_outer_dims().rearrange("(c p r) k -> c p (r k)", p=P, r=ROWS)
+    x_chunks = x.flatten_outer_dims().rearrange("(c p r) k -> c p (r k)", p=P, r=ROWS)
     q_frames = out_0.rearrange("(b h t) d i j -> b t d h (i j)", b=CLIPS, h=HEADS)
     k_frames = out_1.rearrange("(b h t) d i j -> b t d h (i j)", b=CLIPS, h=HEADS)
 
@@ -71,7 +82,7 @@ def tile_costvolumeattention17_pa_t_kernel(tc, x, q_w, k_w, out_0, out_1):
             return flipped
 
         def regroup(flipped):
-            grouped = work.tile([P, BLOCK * PACK], BF16, align_bytes=64)
+            grouped = work.tile([P, CHUNK * PACK], BF16, align_bytes=64)
             nc.scalar.copy(
                 out=grouped[:].bitcast(F32).rearrange("q (r m u) -> q r m u", r=ROWS, u=HALVES),
                 in_=flipped[:].rearrange("q r u m -> q r m u"),
@@ -86,90 +97,101 @@ def tile_costvolumeattention17_pa_t_kernel(tc, x, q_w, k_w, out_0, out_1):
 
         def load(c):
             x_rows[c] = loads.tile([P, ROWS * CHANNELS], BF16, name="x_rows")
-            nc.sync.dma_start(out=x_rows[c][:], in_=x_blocks[c])
+            nc.sync.dma_start(out=x_rows[c][:], in_=x_chunks[c])
 
         def transpose_in(c):
             x_flipped[c] = transpose_words(x_rows[c][:])
 
-        def regroup_block(c):
+        def regroup_chunk(c):
             x_grouped[c] = regroup(x_flipped[c])
 
-        def quantise_block(c):
-            x_codes[c] = work.tile([P, BLOCK], U32, name="x_codes", align_bytes=64)
-            x_scales[c] = work.tile([P, BLOCK], U8, name="x_scales", align_bytes=64)
+        def quantise_chunk(c):
+            x_codes[c] = work.tile([P, CHUNK], U32, name="x_codes", align_bytes=64)
+            x_scales[c] = work.tile([P, CHUNK], U8, name="x_scales", align_bytes=64)
             quantise(x_grouped[c], x_codes[c], x_scales[c])
 
         def multiply(c):
-            products[c] = psum_mx.tile([P, ROWS, KINDS * P], F32, name="products")
-            for r in range(ROWS):
-                tokens = slice(r * P, (r + 1) * P)
-                nc.tensor.matmul_mx(
-                    out=products[c][:, r, :],
-                    lhsT=x_codes[c][:, tokens].bitcast(FP8X4),
-                    lhsT_scale=x_scales[c][:, tokens],
-                    rhs=w_codes[:].bitcast(FP8X4),
-                    rhs_scale=w_scales[:],
-                    start=True,
-                    stop=True,
-                )
+            products[c] = psum_mx.tile([P, KINDS, ROWS, P], F32, name="products")
+            for k in range(kinds_of(c)):
+                for r in range(ROWS):
+                    nc.tensor.matmul_mx(
+                        out=products[c][:, k, r, :],
+                        lhsT=x_codes[c][:, r * P : (r + 1) * P].bitcast(FP8X4),
+                        lhsT_scale=x_scales[c][:, r * P : (r + 1) * P],
+                        rhs=w_codes[:, k * P : (k + 1) * P].bitcast(FP8X4),
+                        rhs_scale=w_scales[:, k * P : (k + 1) * P],
+                        start=True,
+                        stop=True,
+                    )
 
         def square(c):
-            squares[c] = work.tile([P, GROUPS, HEAD_DIM], F32, name="squares")
+            squares[c] = work.tile([P, KINDS, ROWS * HEADS, HEAD_DIM], F32, name="squares")
             nc.scalar.activation(
-                out=squares[c][:].rearrange("p g d -> p (g d)"),
-                in_=products[c][:].rearrange("p r e -> p (r e)"),
+                out=squares[c][:, 0 : kinds_of(c)].rearrange("p k g d -> p (k g d)"),
+                in_=products[c][:, 0 : kinds_of(c)].rearrange("p k r e -> p (k r e)"),
                 func=ACT.Square,
             )
 
         def sum_squares(c):
-            sums[c] = work.tile([P, GROUPS], F32, name="sums")
-            nc.vector.tensor_reduce(out=sums[c][:], in_=squares[c][:], axis=mybir.AxisListType.X, op=ALU.add)
+            sums[c] = work.tile([P, KINDS, ROWS * HEADS], F32, name="sums")
+            nc.vector.tensor_reduce(
+                out=sums[c][:, 0 : kinds_of(c)],
+                in_=squares[c][:, 0 : kinds_of(c)],
+                axis=mybir.AxisListType.X,
+                op=ALU.add,
+            )
 
         def clamp(c):
-            nc.vector.tensor_scalar_max(out=sums[c][:], in0=sums[c][:], scalar1=EPS * EPS)
+            live = sums[c][:, 0 : kinds_of(c)]
+            nc.vector.tensor_scalar_max(out=live, in0=live, scalar1=EPS * EPS)
 
         def invert(c):
-            inverse_norms[c] = work.tile([P, GROUPS], F32, name="inverse_norms")
-            nc.scalar.activation(out=inverse_norms[c][:], in_=sums[c][:], func=ACT.Abs_reciprocal_sqrt)
+            inverse_norms[c] = work.tile([P, KINDS, ROWS * HEADS], F32, name="inverse_norms")
+            nc.scalar.activation(
+                out=inverse_norms[c][:, 0 : kinds_of(c)],
+                in_=sums[c][:, 0 : kinds_of(c)],
+                func=ACT.Abs_reciprocal_sqrt,
+            )
 
         def normalise(c):
-            normalised[c] = work.tile([P, ROWS * KINDS, HEAD_DIM, HEADS], F32, name="normalised")
+            sets = kinds_of(c) * ROWS
+            normalised[c] = work.tile([P, KINDS * ROWS, HEAD_DIM, HEADS], F32, name="normalised")
             nc.vector.tensor_tensor(
-                out=normalised[c][:],
-                in0=products[c][:].rearrange("p r (k h d) -> p (r k) d h", k=KINDS, h=HEADS),
-                in1=inverse_norms[c][:]
-                .rearrange("p (a h) -> p a h", h=HEADS)
+                out=normalised[c][:, 0:sets],
+                in0=products[c][:, 0 : kinds_of(c)].rearrange("p k r (h d) -> p (k r) d h", h=HEADS),
+                in1=inverse_norms[c][:, 0 : kinds_of(c)]
+                .rearrange("p k (r h) -> p (k r) h", h=HEADS)
                 .unsqueeze(2)
-                .to_broadcast([P, ROWS * KINDS, HEAD_DIM, HEADS]),
+                .to_broadcast([P, sets, HEAD_DIM, HEADS]),
                 op=ALU.mult,
             )
 
         def transpose_back(c):
             out_flipped[c] = psum_out.tile([P, KINDS, ROWS, P], F32, name="out_flipped")
-            for r in range(ROWS):
-                for k in range(KINDS):
+            for k in range(kinds_of(c)):
+                for r in range(ROWS):
                     nc.tensor.transpose(
                         out_flipped[c][:, k, r, :],
-                        normalised[c][:, r * KINDS + k, :, :].rearrange("p d h -> p (d h)"),
+                        normalised[c][:, k * ROWS + r, :, :].rearrange("p d h -> p (d h)"),
                         identity[:],
                     )
 
         def stage(c):
             copy = nc.vector.tensor_copy if c % STAGE_ON_VECTOR_EVERY == 0 else nc.scalar.copy
-            for f in range(c * BLOCK // FRAME, ((c + 1) * BLOCK - 1) // FRAME + 1):
-                first = max(c * BLOCK, f * FRAME)
-                last = min((c + 1) * BLOCK, (f + 1) * FRAME)
-                if first == f * FRAME:
+            for f in reversed(frames_of(c)):
+                first = max(c * CHUNK, f * FRAME)
+                last = min((c + 1) * CHUNK, (f + 1) * FRAME)
+                if last == (f + 1) * FRAME:
                     staged[f] = frames.tile([P, KINDS, FRAME], F32, name="staged")
                 copy(
-                    out=staged[f][:, :, first - f * FRAME : last - f * FRAME].rearrange(
+                    out=staged[f][:, 0 : kinds_of_frame(f), first - f * FRAME : last - f * FRAME].rearrange(
                         "e k (m r) -> e k m r", r=ROWS
                     ),
-                    in_=out_flipped[c][:, :, :, (first - c * BLOCK) // ROWS : (last - c * BLOCK) // ROWS].rearrange(
-                        "e k r m -> e k m r"
-                    ),
+                    in_=out_flipped[c][
+                        :, 0 : kinds_of_frame(f), :, (first - c * CHUNK) // ROWS : (last - c * CHUNK) // ROWS
+                    ].rearrange("e k r m -> e k m r"),
                 )
-                if last == (f + 1) * FRAME:
+                if first == f * FRAME:
                     store(f)
 
         def store(f):
@@ -180,26 +202,26 @@ def tile_costvolumeattention17_pa_t_kernel(tc, x, q_w, k_w, out_0, out_1):
             if t == FRAMES_PER_CLIP - 1:
                 nc.sync.dma_start(out=k_frames[b, t], in_=staged[f][:, 1, :])
 
+        def run(step, turn):
+            if 0 <= turn < CHUNKS:
+                step(CHUNKS - 1 - turn)
+
         w_rows = keep.tile([P, KINDS * CHANNELS], BF16)
         nc.scalar.dma_start(out=w_rows[:, 0:CHANNELS], in_=q_w)
         nc.scalar.dma_start(out=w_rows[:, CHANNELS : KINDS * CHANNELS], in_=k_w)
-        for c in range(LOADS_AHEAD):
-            load(c)
+        for turn in range(LOADS_AHEAD):
+            run(load, turn)
         w_codes = keep.tile([P, KINDS * P], U32, align_bytes=64)
         w_scales = keep.tile([P, KINDS * P], U8, align_bytes=64)
         quantise(regroup(transpose_words(w_rows[:])), w_codes, w_scales)
 
-        def run(step, c):
-            if 0 <= c < BLOCKS:
-                step(c)
-
-        for n in range(BLOCKS + LAG_STAGE):
+        for n in range(CHUNKS + LAG_STAGE):
             run(load, n + LOADS_AHEAD)
-            run(quantise_block, n - LAG_QUANTISE)
+            run(quantise_chunk, n - LAG_QUANTISE)
             run(multiply, n - LAG_MULTIPLY)
             run(transpose_in, n)
             run(transpose_back, n - LAG_TRANSPOSE_BACK)
-            run(regroup_block, n - LAG_REGROUP)
+            run(regroup_chunk, n - LAG_REGROUP)
             run(clamp, n - LAG_INVERT)
             run(normalise, n - LAG_NORMALISE)
             run(stage, n - LAG_STAGE)

@@ -27,13 +27,13 @@ EPS = 1e-12
 
 LOADS_AHEAD = 6
 LAG_REGROUP = 1
-LAG_QUANTISE = 2
-LAG_MULTIPLY = 3
-LAG_SUM = 4
-LAG_INVERT = 5
-LAG_NORMALISE = 6
-LAG_TRANSPOSE_BACK = 7
-LAG_STAGE = 8
+LAG_QUANTISE = 1
+LAG_MULTIPLY = 4
+LAG_SUM = 5
+LAG_INVERT = 7
+LAG_NORMALISE = 7
+LAG_TRANSPOSE_BACK = 9
+LAG_STAGE = 10
 STAGE_ON_VECTOR_EVERY = 4
 
 FLOPS = 2 * TOKENS * CHANNELS * KINDS * HEADS * HEAD_DIM
@@ -63,18 +63,21 @@ def tile_costvolumeattention17_pa_t_kernel(tc, x, q_w, k_w, out_0, out_1):
         ctx.enter_context(tc.manual_schedule())
         keep = ctx.enter_context(tc.tile_pool(name="keep", bufs=1))
         loads = ctx.enter_context(tc.tile_pool(name="loads", bufs=LOADS_AHEAD + 2))
-        work = ctx.enter_context(tc.tile_pool(name="work", bufs=3))
+        work = ctx.enter_context(tc.tile_pool(name="work", bufs=4))
         frames = ctx.enter_context(tc.tile_pool(name="frames", bufs=3))
-        psum_in = ctx.enter_context(tc.psum_pool(name="psum_in", bufs=2))
-        psum_mx = ctx.enter_context(tc.psum_pool(name="psum_mx", bufs=4))
-        psum_out = ctx.enter_context(tc.psum_pool(name="psum_out", bufs=2))
+        psum_flip = ctx.enter_context(tc.psum_pool(name="psum_flip", bufs=3))
+        psum_mx = ctx.enter_context(tc.psum_pool(name="psum_mx", bufs=5))
+
+        warm = keep.tile([P, 1], F32)
+        nc.vector.memset(warm[:], 1.0)
+        nc.scalar.activation(out=warm[:], in_=warm[:], func=ACT.Abs_reciprocal_sqrt)
 
         identity = keep.tile([P, P], F32)
         make_identity(nc, identity[:])
 
         def transpose_words(rows):
             words = rows.bitcast(F32)
-            flipped = psum_in.tile([P, ROWS, HALVES, P], F32)
+            flipped = psum_flip.tile([P, ROWS, HALVES, P], F32, name="flipped")
             for r in range(ROWS):
                 for u in range(HALVES):
                     first = (r * HALVES + u) * P
@@ -167,7 +170,7 @@ def tile_costvolumeattention17_pa_t_kernel(tc, x, q_w, k_w, out_0, out_1):
             )
 
         def transpose_back(c):
-            out_flipped[c] = psum_out.tile([P, KINDS, ROWS, P], F32, name="out_flipped")
+            out_flipped[c] = psum_flip.tile([P, KINDS, ROWS, P], F32, name="flipped")
             for k in range(kinds_of(c)):
                 for r in range(ROWS):
                     nc.tensor.transpose(
@@ -217,14 +220,14 @@ def tile_costvolumeattention17_pa_t_kernel(tc, x, q_w, k_w, out_0, out_1):
 
         for n in range(CHUNKS + LAG_STAGE):
             run(load, n + LOADS_AHEAD)
-            run(quantise_chunk, n - LAG_QUANTISE)
+            run(regroup_chunk, n - LAG_REGROUP)
+            run(invert, n - LAG_INVERT)
             run(multiply, n - LAG_MULTIPLY)
+            run(stage, n - LAG_STAGE)
             run(transpose_in, n)
             run(transpose_back, n - LAG_TRANSPOSE_BACK)
-            run(regroup_chunk, n - LAG_REGROUP)
-            run(clamp, n - LAG_INVERT)
-            run(normalise, n - LAG_NORMALISE)
-            run(stage, n - LAG_STAGE)
             run(sum_squares, n - LAG_SUM)
-            run(invert, n - LAG_INVERT)
             run(square, n - LAG_MULTIPLY)
+            run(quantise_chunk, n - LAG_QUANTISE)
+            run(normalise, n - LAG_NORMALISE)
+            run(clamp, n - LAG_SUM)

@@ -35,6 +35,7 @@ LAG_NORMALISE = 7
 LAG_TRANSPOSE_BACK = 9
 LAG_STAGE = 10
 STAGE_ON_VECTOR_EVERY = 4
+PASSES = 2
 
 FLOPS = 2 * TOKENS * CHANNELS * KINDS * HEADS * HEAD_DIM
 
@@ -67,10 +68,6 @@ def tile_costvolumeattention17_pa_t_kernel(tc, x, q_w, k_w, out_0, out_1):
         frames = ctx.enter_context(tc.tile_pool(name="frames", bufs=3))
         psum_flip = ctx.enter_context(tc.psum_pool(name="psum_flip", bufs=3))
         psum_mx = ctx.enter_context(tc.psum_pool(name="psum_mx", bufs=5))
-
-        warm = keep.tile([P, 1], F32)
-        nc.vector.memset(warm[:], 1.0)
-        nc.scalar.activation(out=warm[:], in_=warm[:], func=ACT.Abs_reciprocal_sqrt)
 
         identity = keep.tile([P, P], F32)
         make_identity(nc, identity[:])
@@ -114,58 +111,55 @@ def tile_costvolumeattention17_pa_t_kernel(tc, x, q_w, k_w, out_0, out_1):
             quantise(x_grouped[c], x_codes[c], x_scales[c])
 
         def multiply(c):
-            products[c] = psum_mx.tile([P, KINDS, ROWS, P], F32, name="products")
-            for k in range(kinds_of(c)):
-                for r in range(ROWS):
+            products[c] = psum_mx.tile([P, ROWS, KINDS, P], F32, name="products")
+            for r in range(ROWS):
+                for repeat in range(PASSES):
                     nc.tensor.matmul_mx(
-                        out=products[c][:, k, r, :],
+                        out=products[c][:, r, :, :].rearrange("p k e -> p (k e)"),
                         lhsT=x_codes[c][:, r * P : (r + 1) * P].bitcast(FP8X4),
                         lhsT_scale=x_scales[c][:, r * P : (r + 1) * P],
-                        rhs=w_codes[:, k * P : (k + 1) * P].bitcast(FP8X4),
-                        rhs_scale=w_scales[:, k * P : (k + 1) * P],
+                        rhs=w_codes[:].bitcast(FP8X4),
+                        rhs_scale=w_scales[:],
                         start=True,
                         stop=True,
                     )
 
         def square(c):
-            squares[c] = work.tile([P, KINDS, ROWS * HEADS, HEAD_DIM], F32, name="squares")
+            squares[c] = work.tile([P, ROWS, KINDS, P], F32, name="squares")
             nc.scalar.activation(
-                out=squares[c][:, 0 : kinds_of(c)].rearrange("p k g d -> p (k g d)"),
-                in_=products[c][:, 0 : kinds_of(c)].rearrange("p k r e -> p (k r e)"),
+                out=squares[c][:, :, 0 : kinds_of(c)].rearrange("p r k e -> p r (k e)"),
+                in_=products[c][:, :, 0 : kinds_of(c)].rearrange("p r k e -> p r (k e)"),
                 func=ACT.Square,
             )
 
         def sum_squares(c):
-            sums[c] = work.tile([P, KINDS, ROWS * HEADS], F32, name="sums")
+            sums[c] = work.tile([P, ROWS * KINDS, HEADS], F32, name="sums")
             nc.vector.tensor_reduce(
-                out=sums[c][:, 0 : kinds_of(c)],
-                in_=squares[c][:, 0 : kinds_of(c)],
+                out=sums[c][:, 0 : ROWS * kinds_of(c)].rearrange("p (r k) h -> p r (k h)", r=ROWS),
+                in_=squares[c][:, :, 0 : kinds_of(c)].rearrange("p r k (h d) -> p r (k h) d", h=HEADS),
                 axis=mybir.AxisListType.X,
                 op=ALU.add,
             )
 
         def clamp(c):
-            live = sums[c][:, 0 : kinds_of(c)]
+            live = sums[c][:, 0 : ROWS * kinds_of(c)]
             nc.vector.tensor_scalar_max(out=live, in0=live, scalar1=EPS * EPS)
 
         def invert(c):
-            inverse_norms[c] = work.tile([P, KINDS, ROWS * HEADS], F32, name="inverse_norms")
+            inverse_norms[c] = work.tile([P, ROWS * KINDS, HEADS], F32, name="inverse_norms")
             nc.scalar.activation(
-                out=inverse_norms[c][:, 0 : kinds_of(c)],
-                in_=sums[c][:, 0 : kinds_of(c)],
+                out=inverse_norms[c][:, 0 : ROWS * kinds_of(c)],
+                in_=sums[c][:, 0 : ROWS * kinds_of(c)],
                 func=ACT.Abs_reciprocal_sqrt,
             )
 
         def normalise(c):
-            sets = kinds_of(c) * ROWS
-            normalised[c] = work.tile([P, KINDS * ROWS, HEAD_DIM, HEADS], F32, name="normalised")
+            sets = ROWS * kinds_of(c)
+            normalised[c] = work.tile([P, ROWS * KINDS, HEAD_DIM, HEADS], F32, name="normalised")
             nc.vector.tensor_tensor(
                 out=normalised[c][:, 0:sets],
-                in0=products[c][:, 0 : kinds_of(c)].rearrange("p k r (h d) -> p (k r) d h", h=HEADS),
-                in1=inverse_norms[c][:, 0 : kinds_of(c)]
-                .rearrange("p k (r h) -> p (k r) h", h=HEADS)
-                .unsqueeze(2)
-                .to_broadcast([P, sets, HEAD_DIM, HEADS]),
+                in0=products[c][:, :, 0 : kinds_of(c)].rearrange("p r k (h d) -> p (r k) d h", h=HEADS),
+                in1=inverse_norms[c][:, 0:sets].unsqueeze(2).to_broadcast([P, sets, HEAD_DIM, HEADS]),
                 op=ALU.mult,
             )
 
@@ -175,7 +169,7 @@ def tile_costvolumeattention17_pa_t_kernel(tc, x, q_w, k_w, out_0, out_1):
                 for r in range(ROWS):
                     nc.tensor.transpose(
                         out_flipped[c][:, k, r, :],
-                        normalised[c][:, k * ROWS + r, :, :].rearrange("p d h -> p (d h)"),
+                        normalised[c][:, r * kinds_of(c) + k, :, :].rearrange("p d h -> p (d h)"),
                         identity[:],
                     )
 
@@ -214,6 +208,9 @@ def tile_costvolumeattention17_pa_t_kernel(tc, x, q_w, k_w, out_0, out_1):
         nc.scalar.dma_start(out=w_rows[:, CHANNELS : KINDS * CHANNELS], in_=k_w)
         for turn in range(LOADS_AHEAD):
             run(load, turn)
+        warm = keep.tile([P, 1], F32)
+        nc.vector.memset(warm[:], 1.0)
+        nc.scalar.activation(out=warm[:], in_=warm[:], func=ACT.Abs_reciprocal_sqrt)
         w_codes = keep.tile([P, KINDS * P], U32, align_bytes=64)
         w_scales = keep.tile([P, KINDS * P], U8, align_bytes=64)
         quantise(regroup(transpose_words(w_rows[:])), w_codes, w_scales)

@@ -27,15 +27,16 @@ EPS = 1e-12
 
 LOADS_AHEAD = 6
 LAG_REGROUP = 1
-LAG_QUANTISE = 1
+LAG_QUANTISE = 2
 LAG_MULTIPLY = 4
 LAG_SUM = 5
-LAG_INVERT = 7
+LAG_INVERT = 6
 LAG_NORMALISE = 7
-LAG_TRANSPOSE_BACK = 9
-LAG_STAGE = 10
-STAGE_ON_VECTOR_EVERY = 4
-PASSES = 2
+LAG_TRANSPOSE_BACK = 8
+LAG_STAGE = 9
+LAG_HEAD_SUM = 6
+LAG_HEAD_SCALE = 7
+BY_CHANNEL_EVERY = 3
 
 FLOPS = 2 * TOKENS * CHANNELS * KINDS * HEADS * HEAD_DIM
 
@@ -52,11 +53,15 @@ def kinds_of(c):
     return max(kinds_of_frame(f) for f in frames_of(c))
 
 
+def by_channel(c):
+    return c % BY_CHANNEL_EVERY == 1 and all(kinds_of_frame(f) == KINDS for f in frames_of(c))
+
+
 def tile_costvolumeattention17_pa_t_kernel(tc, x, q_w, k_w, out_0, out_1):
     nc = tc.nc
     assert TOKENS == CHUNKS * CHUNK
 
-    x_chunks = x.flatten_outer_dims().rearrange("(c p r) k -> c p (r k)", p=P, r=ROWS)
+    x_chunks = x.flatten_outer_dims().rearrange("(c r p) k -> c p r k", p=P, r=ROWS)
     q_frames = out_0.rearrange("(b h t) d i j -> b t d h (i j)", b=CLIPS, h=HEADS)
     k_frames = out_1.rearrange("(b h t) d i j -> b t d h (i j)", b=CLIPS, h=HEADS)
 
@@ -65,8 +70,8 @@ def tile_costvolumeattention17_pa_t_kernel(tc, x, q_w, k_w, out_0, out_1):
         keep = ctx.enter_context(tc.tile_pool(name="keep", bufs=1))
         loads = ctx.enter_context(tc.tile_pool(name="loads", bufs=LOADS_AHEAD + 2))
         work = ctx.enter_context(tc.tile_pool(name="work", bufs=4))
-        frames = ctx.enter_context(tc.tile_pool(name="frames", bufs=3))
-        psum_flip = ctx.enter_context(tc.psum_pool(name="psum_flip", bufs=3))
+        frames = ctx.enter_context(tc.tile_pool(name="frames", bufs=4))
+        psum_short = ctx.enter_context(tc.psum_pool(name="psum_short", bufs=3))
         psum_mx = ctx.enter_context(tc.psum_pool(name="psum_mx", bufs=5))
 
         identity = keep.tile([P, P], F32)
@@ -74,7 +79,7 @@ def tile_costvolumeattention17_pa_t_kernel(tc, x, q_w, k_w, out_0, out_1):
 
         def transpose_words(rows):
             words = rows.bitcast(F32)
-            flipped = psum_flip.tile([P, ROWS, HALVES, P], F32, name="flipped")
+            flipped = psum_short.tile([P, ROWS, HALVES, P], F32, name="short")
             for r in range(ROWS):
                 for u in range(HALVES):
                     first = (r * HALVES + u) * P
@@ -82,22 +87,34 @@ def tile_costvolumeattention17_pa_t_kernel(tc, x, q_w, k_w, out_0, out_1):
             return flipped
 
         def regroup(flipped):
-            grouped = work.tile([P, CHUNK * PACK], BF16, align_bytes=64)
+            grouped = work.tile([P, CHUNK * PACK], BF16, name="grouped", align_bytes=64)
             nc.scalar.copy(
                 out=grouped[:].bitcast(F32).rearrange("q (r m u) -> q r m u", r=ROWS, u=HALVES),
                 in_=flipped[:].rearrange("q r u m -> q r m u"),
             )
             return grouped
 
+        def regroup_weights(flipped):
+            grouped = work.tile([P, CHUNK * PACK], BF16, name="grouped", align_bytes=64)
+            for k in range(KINDS):
+                nc.scalar.copy(
+                    out=grouped[:, k * P * PACK : (k + 1) * P * PACK]
+                    .bitcast(F32)
+                    .rearrange("q (d h u) -> q d h u", h=HEADS, u=HALVES),
+                    in_=flipped[:, k, :, :].rearrange("q u (h d) -> q d h u", h=HEADS),
+                )
+            return grouped
+
         def quantise(grouped, codes, scales):
             nc.vector.quantize_mx(out=codes[:].bitcast(FP8X4), scales=scales[:], in_=grouped[:])
 
         x_rows, x_flipped, x_grouped, x_codes, x_scales = {}, {}, {}, {}, {}
-        products, squares, sums, inverse_norms, normalised, out_flipped, staged = {}, {}, {}, {}, {}, {}, {}
+        products, squares, sums, inverse_norms, normalised, out_flipped = {}, {}, {}, {}, {}, {}
+        staged, missing = {}, {}
 
         def load(c):
             x_rows[c] = loads.tile([P, ROWS * CHANNELS], BF16, name="x_rows")
-            nc.sync.dma_start(out=x_rows[c][:], in_=x_chunks[c])
+            nc.sync.dma_start(out=x_rows[c][:].rearrange("p (r k) -> p r k", r=ROWS), in_=x_chunks[c])
 
         def transpose_in(c):
             x_flipped[c] = transpose_words(x_rows[c][:])
@@ -111,34 +128,51 @@ def tile_costvolumeattention17_pa_t_kernel(tc, x, q_w, k_w, out_0, out_1):
             quantise(x_grouped[c], x_codes[c], x_scales[c])
 
         def multiply(c):
-            products[c] = psum_mx.tile([P, ROWS, KINDS, P], F32, name="products")
-            for r in range(ROWS):
-                for repeat in range(PASSES):
+            if by_channel(c):
+                products[c] = psum_mx.tile([P, KINDS, CHUNK], F32, name="products")
+                for k in range(KINDS):
                     nc.tensor.matmul_mx(
-                        out=products[c][:, r, :, :].rearrange("p k e -> p (k e)"),
-                        lhsT=x_codes[c][:, r * P : (r + 1) * P].bitcast(FP8X4),
-                        lhsT_scale=x_scales[c][:, r * P : (r + 1) * P],
-                        rhs=w_codes[:].bitcast(FP8X4),
-                        rhs_scale=w_scales[:],
+                        out=products[c][:, k, :],
+                        lhsT=w_codes[:, k * P : (k + 1) * P].bitcast(FP8X4),
+                        lhsT_scale=w_scales[:, k * P : (k + 1) * P],
+                        rhs=x_codes[c][:].bitcast(FP8X4),
+                        rhs_scale=x_scales[c][:],
                         start=True,
                         stop=True,
                     )
+                return
+            products[c] = psum_mx.tile([P, ROWS, KINDS, P], F32, name="products")
+            width = kinds_of(c) * P
+            for r in range(ROWS):
+                nc.tensor.matmul_mx(
+                    out=products[c][:, r, 0 : kinds_of(c), :].rearrange("p k e -> p (k e)"),
+                    lhsT=x_codes[c][:, r * P : (r + 1) * P].bitcast(FP8X4),
+                    lhsT_scale=x_scales[c][:, r * P : (r + 1) * P],
+                    rhs=w_codes[:, 0:width].bitcast(FP8X4),
+                    rhs_scale=w_scales[:, 0:width],
+                    start=True,
+                    stop=True,
+                )
 
         def square(c):
-            squares[c] = work.tile([P, ROWS, KINDS, P], F32, name="squares")
+            if by_channel(c):
+                squares[c] = work.tile([P, KINDS, CHUNK], F32, name="squares")
+                nc.scalar.activation(out=squares[c][:], in_=products[c][:], func=ACT.Square)
+                return
+            sets = ROWS * kinds_of(c)
+            squares[c] = work.tile([P, ROWS * KINDS, HEADS, HEAD_DIM], F32, name="squares")
             nc.scalar.activation(
-                out=squares[c][:, :, 0 : kinds_of(c)].rearrange("p r k e -> p r (k e)"),
-                in_=products[c][:, :, 0 : kinds_of(c)].rearrange("p r k e -> p r (k e)"),
+                out=squares[c][:, 0:sets],
+                in_=products[c][:, :, 0 : kinds_of(c)].rearrange("p r k (d h) -> p (r k) h d", h=HEADS),
                 func=ACT.Square,
             )
 
+
         def sum_squares(c):
+            sets = ROWS * kinds_of(c)
             sums[c] = work.tile([P, ROWS * KINDS, HEADS], F32, name="sums")
             nc.vector.tensor_reduce(
-                out=sums[c][:, 0 : ROWS * kinds_of(c)].rearrange("p (r k) h -> p r (k h)", r=ROWS),
-                in_=squares[c][:, :, 0 : kinds_of(c)].rearrange("p r k (h d) -> p r (k h) d", h=HEADS),
-                axis=mybir.AxisListType.X,
-                op=ALU.add,
+                out=sums[c][:, 0:sets], in_=squares[c][:, 0:sets], axis=mybir.AxisListType.X, op=ALU.add
             )
 
         def clamp(c):
@@ -146,49 +180,78 @@ def tile_costvolumeattention17_pa_t_kernel(tc, x, q_w, k_w, out_0, out_1):
             nc.vector.tensor_scalar_max(out=live, in0=live, scalar1=EPS * EPS)
 
         def invert(c):
+            sets = ROWS * kinds_of(c)
             inverse_norms[c] = work.tile([P, ROWS * KINDS, HEADS], F32, name="inverse_norms")
-            nc.scalar.activation(
-                out=inverse_norms[c][:, 0 : ROWS * kinds_of(c)],
-                in_=sums[c][:, 0 : ROWS * kinds_of(c)],
-                func=ACT.Abs_reciprocal_sqrt,
-            )
+            nc.scalar.activation(out=inverse_norms[c][:, 0:sets], in_=sums[c][:, 0:sets], func=ACT.Abs_reciprocal_sqrt)
 
         def normalise(c):
             sets = ROWS * kinds_of(c)
             normalised[c] = work.tile([P, ROWS * KINDS, HEAD_DIM, HEADS], F32, name="normalised")
             nc.vector.tensor_tensor(
                 out=normalised[c][:, 0:sets],
-                in0=products[c][:, :, 0 : kinds_of(c)].rearrange("p r k (h d) -> p (r k) d h", h=HEADS),
+                in0=products[c][:, :, 0 : kinds_of(c)].rearrange("p r k (d h) -> p (r k) d h", h=HEADS),
                 in1=inverse_norms[c][:, 0:sets].unsqueeze(2).to_broadcast([P, sets, HEAD_DIM, HEADS]),
                 op=ALU.mult,
             )
 
         def transpose_back(c):
-            out_flipped[c] = psum_flip.tile([P, KINDS, ROWS, P], F32, name="flipped")
+            out_flipped[c] = psum_short.tile([P, KINDS, CHUNK], F32, name="short")
             for k in range(kinds_of(c)):
                 for r in range(ROWS):
                     nc.tensor.transpose(
-                        out_flipped[c][:, k, r, :],
+                        out_flipped[c][:, k, r * P : (r + 1) * P],
                         normalised[c][:, r * kinds_of(c) + k, :, :].rearrange("p d h -> p (d h)"),
                         identity[:],
                     )
 
         def stage(c):
-            copy = nc.vector.tensor_copy if c % STAGE_ON_VECTOR_EVERY == 0 else nc.scalar.copy
+            copy = nc.scalar.copy if c % BY_CHANNEL_EVERY == 0 else nc.vector.tensor_copy
+            place(c, lambda out, kinds, span: copy(out=out, in_=out_flipped[c][:, kinds, span]))
+
+
+        def sum_heads(c):
+            sums[c] = psum_short.tile([P, KINDS, CHUNK], F32, name="short")
+            nc.tensor.matmul(
+                sums[c][:].rearrange("e k n -> e (k n)"),
+                lhsT=same_head[:],
+                rhs=squares[c][:].rearrange("e k n -> e (k n)"),
+                start=True,
+                stop=True,
+            )
+
+        def invert_heads(c):
+            inverse_norms[c] = work.tile([P, KINDS, CHUNK], F32, name="wide_inverse_norms")
+            nc.scalar.activation(out=inverse_norms[c][:], in_=sums[c][:], func=ACT.Abs_reciprocal_sqrt)
+
+        def scale_heads(c):
+            place(
+                c,
+                lambda out, kinds, span: nc.vector.scalar_tensor_tensor(
+                    out=out,
+                    in0=inverse_norms[c][:, kinds, span],
+                    scalar=1.0 / EPS,
+                    in1=products[c][:, kinds, span],
+                    op0=ALU.min,
+                    op1=ALU.mult,
+                ),
+            )
+
+
+        def place(c, write):
             for f in reversed(frames_of(c)):
                 first = max(c * CHUNK, f * FRAME)
                 last = min((c + 1) * CHUNK, (f + 1) * FRAME)
-                if last == (f + 1) * FRAME:
+                if f not in staged:
                     staged[f] = frames.tile([P, KINDS, FRAME], F32, name="staged")
-                copy(
-                    out=staged[f][:, 0 : kinds_of_frame(f), first - f * FRAME : last - f * FRAME].rearrange(
-                        "e k (m r) -> e k m r", r=ROWS
-                    ),
-                    in_=out_flipped[c][
-                        :, 0 : kinds_of_frame(f), :, (first - c * CHUNK) // ROWS : (last - c * CHUNK) // ROWS
-                    ].rearrange("e k r m -> e k m r"),
+                    missing[f] = FRAME
+                kinds = slice(0, kinds_of_frame(f))
+                write(
+                    staged[f][:, kinds, first - f * FRAME : last - f * FRAME],
+                    kinds,
+                    slice(first - c * CHUNK, last - c * CHUNK),
                 )
-                if first == f * FRAME:
+                missing[f] -= last - first
+                if missing[f] == 0:
                     store(f)
 
         def store(f):
@@ -199,9 +262,10 @@ def tile_costvolumeattention17_pa_t_kernel(tc, x, q_w, k_w, out_0, out_1):
             if t == FRAMES_PER_CLIP - 1:
                 nc.sync.dma_start(out=k_frames[b, t], in_=staged[f][:, 1, :])
 
-        def run(step, turn):
-            if 0 <= turn < CHUNKS:
-                step(CHUNKS - 1 - turn)
+        def run(step, turn, which=None):
+            c = CHUNKS - 1 - turn
+            if 0 <= c < CHUNKS and which in (None, by_channel(c)):
+                step(c)
 
         w_rows = keep.tile([P, KINDS * CHANNELS], BF16)
         nc.scalar.dma_start(out=w_rows[:, 0:CHANNELS], in_=q_w)
@@ -211,20 +275,32 @@ def tile_costvolumeattention17_pa_t_kernel(tc, x, q_w, k_w, out_0, out_1):
         warm = keep.tile([P, 1], F32)
         nc.vector.memset(warm[:], 1.0)
         nc.scalar.activation(out=warm[:], in_=warm[:], func=ACT.Abs_reciprocal_sqrt)
+        head_of = keep.tile([P, HEADS], F32)
+        same_head = keep.tile([P, P], F32)
+        nc.vector.tensor_reduce(
+            out=head_of[:], in_=identity[:].rearrange("e (d h) -> e h d", h=HEADS), axis=mybir.AxisListType.X, op=ALU.add
+        )
+        nc.vector.tensor_copy(
+            out=same_head[:].rearrange("e (d h) -> e d h", h=HEADS),
+            in_=head_of[:].unsqueeze(1).to_broadcast([P, HEAD_DIM, HEADS]),
+        )
         w_codes = keep.tile([P, KINDS * P], U32, align_bytes=64)
         w_scales = keep.tile([P, KINDS * P], U8, align_bytes=64)
-        quantise(regroup(transpose_words(w_rows[:])), w_codes, w_scales)
+        quantise(regroup_weights(transpose_words(w_rows[:])), w_codes, w_scales)
 
         for n in range(CHUNKS + LAG_STAGE):
             run(load, n + LOADS_AHEAD)
+            run(stage, n - LAG_STAGE, False)
+            run(normalise, n - LAG_NORMALISE, False)
+            run(sum_squares, n - LAG_SUM, False)
             run(regroup_chunk, n - LAG_REGROUP)
-            run(invert, n - LAG_INVERT)
+            run(scale_heads, n - LAG_HEAD_SCALE, True)
             run(multiply, n - LAG_MULTIPLY)
-            run(stage, n - LAG_STAGE)
-            run(transpose_in, n)
-            run(transpose_back, n - LAG_TRANSPOSE_BACK)
-            run(sum_squares, n - LAG_SUM)
+            run(invert, n - LAG_INVERT, False)
             run(square, n - LAG_MULTIPLY)
             run(quantise_chunk, n - LAG_QUANTISE)
-            run(normalise, n - LAG_NORMALISE)
-            run(clamp, n - LAG_SUM)
+            run(sum_heads, n - LAG_HEAD_SUM, True)
+            run(invert_heads, n - LAG_HEAD_SUM, True)
+            run(clamp, n - LAG_SUM, False)
+            run(transpose_back, n - LAG_TRANSPOSE_BACK, False)
+            run(transpose_in, n)

@@ -27,16 +27,17 @@ EPS = 1e-12
 
 LOADS_AHEAD = 6
 LAG_REGROUP = 1
-LAG_QUANTISE = 2
+LAG_QUANTISE = 1
 LAG_MULTIPLY = 4
 LAG_SUM = 5
 LAG_INVERT = 6
 LAG_NORMALISE = 7
-LAG_TRANSPOSE_BACK = 8
+LAG_TRANSPOSE_BACK = 9
 LAG_STAGE = 9
 LAG_HEAD_SUM = 6
 LAG_HEAD_SCALE = 7
 BY_CHANNEL_EVERY = 3
+LAST_BY_CHANNEL = 3
 
 FLOPS = 2 * TOKENS * CHANNELS * KINDS * HEADS * HEAD_DIM
 
@@ -54,7 +55,8 @@ def kinds_of(c):
 
 
 def by_channel(c):
-    return c % BY_CHANNEL_EVERY == 1 and all(kinds_of_frame(f) == KINDS for f in frames_of(c))
+    wanted = c % BY_CHANNEL_EVERY == 1 or c < LAST_BY_CHANNEL
+    return wanted and all(kinds_of_frame(f) == kinds_of(c) for f in frames_of(c))
 
 
 def tile_costvolumeattention17_pa_t_kernel(tc, x, q_w, k_w, out_0, out_1):
@@ -71,8 +73,8 @@ def tile_costvolumeattention17_pa_t_kernel(tc, x, q_w, k_w, out_0, out_1):
         loads = ctx.enter_context(tc.tile_pool(name="loads", bufs=LOADS_AHEAD + 2))
         work = ctx.enter_context(tc.tile_pool(name="work", bufs=4))
         frames = ctx.enter_context(tc.tile_pool(name="frames", bufs=4))
-        psum_short = ctx.enter_context(tc.psum_pool(name="psum_short", bufs=3))
-        psum_mx = ctx.enter_context(tc.psum_pool(name="psum_mx", bufs=5))
+        psum_short = ctx.enter_context(tc.psum_pool(name="psum_short", bufs=4))
+        psum_mx = ctx.enter_context(tc.psum_pool(name="psum_mx", bufs=4))
 
         identity = keep.tile([P, P], F32)
         make_identity(nc, identity[:])
@@ -130,7 +132,7 @@ def tile_costvolumeattention17_pa_t_kernel(tc, x, q_w, k_w, out_0, out_1):
         def multiply(c):
             if by_channel(c):
                 products[c] = psum_mx.tile([P, KINDS, CHUNK], F32, name="products")
-                for k in range(KINDS):
+                for k in range(kinds_of(c)):
                     nc.tensor.matmul_mx(
                         out=products[c][:, k, :],
                         lhsT=w_codes[:, k * P : (k + 1) * P].bitcast(FP8X4),
@@ -157,7 +159,8 @@ def tile_costvolumeattention17_pa_t_kernel(tc, x, q_w, k_w, out_0, out_1):
         def square(c):
             if by_channel(c):
                 squares[c] = work.tile([P, KINDS, CHUNK], F32, name="squares")
-                nc.scalar.activation(out=squares[c][:], in_=products[c][:], func=ACT.Square)
+                live = slice(0, kinds_of(c))
+                nc.scalar.activation(out=squares[c][:, live], in_=products[c][:, live], func=ACT.Square)
                 return
             sets = ROWS * kinds_of(c)
             squares[c] = work.tile([P, ROWS * KINDS, HEADS, HEAD_DIM], F32, name="squares")
@@ -205,23 +208,24 @@ def tile_costvolumeattention17_pa_t_kernel(tc, x, q_w, k_w, out_0, out_1):
                     )
 
         def stage(c):
-            copy = nc.scalar.copy if c % BY_CHANNEL_EVERY == 0 else nc.vector.tensor_copy
+            copy = nc.scalar.copy if c % BY_CHANNEL_EVERY == 2 else nc.vector.tensor_copy
             place(c, lambda out, kinds, span: copy(out=out, in_=out_flipped[c][:, kinds, span]))
 
 
         def sum_heads(c):
             sums[c] = psum_short.tile([P, KINDS, CHUNK], F32, name="short")
             nc.tensor.matmul(
-                sums[c][:].rearrange("e k n -> e (k n)"),
+                sums[c][:, 0 : kinds_of(c)].rearrange("e k n -> e (k n)"),
                 lhsT=same_head[:],
-                rhs=squares[c][:].rearrange("e k n -> e (k n)"),
+                rhs=squares[c][:, 0 : kinds_of(c)].rearrange("e k n -> e (k n)"),
                 start=True,
                 stop=True,
             )
 
         def invert_heads(c):
             inverse_norms[c] = work.tile([P, KINDS, CHUNK], F32, name="wide_inverse_norms")
-            nc.scalar.activation(out=inverse_norms[c][:], in_=sums[c][:], func=ACT.Abs_reciprocal_sqrt)
+            live = slice(0, kinds_of(c))
+            nc.scalar.activation(out=inverse_norms[c][:, live], in_=sums[c][:, live], func=ACT.Abs_reciprocal_sqrt)
 
         def scale_heads(c):
             place(
@@ -290,17 +294,17 @@ def tile_costvolumeattention17_pa_t_kernel(tc, x, q_w, k_w, out_0, out_1):
 
         for n in range(CHUNKS + LAG_STAGE):
             run(load, n + LOADS_AHEAD)
-            run(stage, n - LAG_STAGE, False)
-            run(normalise, n - LAG_NORMALISE, False)
-            run(sum_squares, n - LAG_SUM, False)
-            run(regroup_chunk, n - LAG_REGROUP)
             run(scale_heads, n - LAG_HEAD_SCALE, True)
-            run(multiply, n - LAG_MULTIPLY)
-            run(invert, n - LAG_INVERT, False)
-            run(square, n - LAG_MULTIPLY)
-            run(quantise_chunk, n - LAG_QUANTISE)
-            run(sum_heads, n - LAG_HEAD_SUM, True)
-            run(invert_heads, n - LAG_HEAD_SUM, True)
-            run(clamp, n - LAG_SUM, False)
             run(transpose_back, n - LAG_TRANSPOSE_BACK, False)
+            run(regroup_chunk, n - LAG_REGROUP)
+            run(sum_heads, n - LAG_HEAD_SUM, True)
+            run(multiply, n - LAG_MULTIPLY)
+            run(stage, n - LAG_STAGE, False)
+            run(invert_heads, n - LAG_HEAD_SUM, True)
+            run(normalise, n - LAG_NORMALISE, False)
+            run(invert, n - LAG_INVERT, False)
+            run(sum_squares, n - LAG_SUM, False)
+            run(quantise_chunk, n - LAG_QUANTISE)
             run(transpose_in, n)
+            run(square, n - LAG_MULTIPLY)
+            run(clamp, n - LAG_SUM, False)

@@ -38,6 +38,7 @@ LAG_HEAD_SUM = 6
 LAG_HEAD_SCALE = 7
 BY_CHANNEL_EVERY = 3
 LAST_BY_CHANNEL = 3
+LAST_FRAMES = 2
 
 FLOPS = 2 * TOKENS * CHANNELS * KINDS * HEADS * HEAD_DIM
 
@@ -72,7 +73,6 @@ def tile_costvolumeattention17_pa_t_kernel(tc, x, q_w, k_w, out_0, out_1):
         keep = ctx.enter_context(tc.tile_pool(name="keep", bufs=1))
         loads = ctx.enter_context(tc.tile_pool(name="loads", bufs=LOADS_AHEAD + 2))
         work = ctx.enter_context(tc.tile_pool(name="work", bufs=4))
-        frames = ctx.enter_context(tc.tile_pool(name="frames", bufs=4))
         psum_short = ctx.enter_context(tc.psum_pool(name="psum_short", bufs=4))
         psum_mx = ctx.enter_context(tc.psum_pool(name="psum_mx", bufs=4))
 
@@ -112,7 +112,8 @@ def tile_costvolumeattention17_pa_t_kernel(tc, x, q_w, k_w, out_0, out_1):
 
         x_rows, x_flipped, x_grouped, x_codes, x_scales = {}, {}, {}, {}, {}
         products, squares, sums, inverse_norms, normalised, out_flipped = {}, {}, {}, {}, {}, {}
-        staged, missing = {}, {}
+        outputs = keep.tile([P, KINDS, TOKENS], F32)
+        missing = {f: FRAME for f in range(FRAMES)}
 
         def load(c):
             x_rows[c] = loads.tile([P, ROWS * CHANNELS], BF16, name="x_rows")
@@ -209,7 +210,7 @@ def tile_costvolumeattention17_pa_t_kernel(tc, x, q_w, k_w, out_0, out_1):
 
         def stage(c):
             copy = nc.scalar.copy if c % BY_CHANNEL_EVERY == 2 else nc.vector.tensor_copy
-            place(c, lambda out, kinds, span: copy(out=out, in_=out_flipped[c][:, kinds, span]))
+            place(c, lambda out, kinds: copy(out=out, in_=out_flipped[c][:, kinds]))
 
 
         def sum_heads(c):
@@ -230,11 +231,11 @@ def tile_costvolumeattention17_pa_t_kernel(tc, x, q_w, k_w, out_0, out_1):
         def scale_heads(c):
             place(
                 c,
-                lambda out, kinds, span: nc.vector.scalar_tensor_tensor(
+                lambda out, kinds: nc.vector.scalar_tensor_tensor(
                     out=out,
-                    in0=inverse_norms[c][:, kinds, span],
+                    in0=inverse_norms[c][:, kinds],
                     scalar=1.0 / EPS,
-                    in1=products[c][:, kinds, span],
+                    in1=products[c][:, kinds],
                     op0=ALU.min,
                     op1=ALU.mult,
                 ),
@@ -242,29 +243,25 @@ def tile_costvolumeattention17_pa_t_kernel(tc, x, q_w, k_w, out_0, out_1):
 
 
         def place(c, write):
-            for f in reversed(frames_of(c)):
-                first = max(c * CHUNK, f * FRAME)
-                last = min((c + 1) * CHUNK, (f + 1) * FRAME)
-                if f not in staged:
-                    staged[f] = frames.tile([P, KINDS, FRAME], F32, name="staged")
-                    missing[f] = FRAME
-                kinds = slice(0, kinds_of_frame(f))
-                write(
-                    staged[f][:, kinds, first - f * FRAME : last - f * FRAME],
-                    kinds,
-                    slice(first - c * CHUNK, last - c * CHUNK),
-                )
-                missing[f] -= last - first
+            kinds = slice(0, kinds_of(c))
+            write(outputs[:, kinds, c * CHUNK : (c + 1) * CHUNK], kinds)
+            for f in frames_of(c):
+                missing[f] -= min((c + 1) * CHUNK, (f + 1) * FRAME) - max(c * CHUNK, f * FRAME)
+                head = -f * FRAME % CHUNK or CHUNK
+                if f < LAST_FRAMES and missing[f] == head:
+                    store(f, head, FRAME)
                 if missing[f] == 0:
-                    store(f)
+                    store(f, 0, head if f < LAST_FRAMES else FRAME)
 
-        def store(f):
+        def store(f, first, last):
             b, t = divmod(f, FRAMES_PER_CLIP)
-            nc.sync.dma_start(out=q_frames[b, t], in_=staged[f][:, 0, :])
+            span = slice(first, last)
+            results = outputs[:, :, f * FRAME + first : f * FRAME + last]
+            nc.sync.dma_start(out=q_frames[b, t][:, :, span], in_=results[:, 0])
             if t > 0:
-                nc.sync.dma_start(out=k_frames[b, t - 1], in_=staged[f][:, 1, :])
+                nc.sync.dma_start(out=k_frames[b, t - 1][:, :, span], in_=results[:, 1])
             if t == FRAMES_PER_CLIP - 1:
-                nc.sync.dma_start(out=k_frames[b, t], in_=staged[f][:, 1, :])
+                nc.sync.dma_start(out=k_frames[b, t][:, :, span], in_=results[:, 1])
 
         def run(step, turn, which=None):
             c = CHUNKS - 1 - turn
@@ -272,8 +269,8 @@ def tile_costvolumeattention17_pa_t_kernel(tc, x, q_w, k_w, out_0, out_1):
                 step(c)
 
         w_rows = keep.tile([P, KINDS * CHANNELS], BF16)
-        nc.scalar.dma_start(out=w_rows[:, 0:CHANNELS], in_=q_w)
-        nc.scalar.dma_start(out=w_rows[:, CHANNELS : KINDS * CHANNELS], in_=k_w)
+        nc.sync.dma_start(out=w_rows[:, 0:CHANNELS], in_=q_w)
+        nc.sync.dma_start(out=w_rows[:, CHANNELS : KINDS * CHANNELS], in_=k_w)
         for turn in range(LOADS_AHEAD):
             run(load, turn)
         warm = keep.tile([P, 1], F32)

from contextlib import ExitStack

import concourse.mybir as mybir
from concourse.masks import make_identity

F32 = mybir.dt.float32
BF16 = mybir.dt.bfloat16
U32 = mybir.dt.uint32
U8 = mybir.dt.uint8
FP8X4 = mybir.dt.float8_e4m3fn_x4
ACT = mybir.ActivationFunctionType
ALU = mybir.AluOpType

P = 128
CLIPS, FRAMES_PER_CLIP, FRAME = 2, 8, 28 * 28
FRAMES = CLIPS * FRAMES_PER_CLIP
TOKENS = FRAMES * FRAME
CHANNELS = 512
PACK = 4
HALVES = 2
KINDS = 2
HEADS, HEAD_DIM = 8, 16
ROWS = 2
CHUNK = ROWS * P
CHUNKS = TOKENS // CHUNK
EPS = 1e-12

LOADS_AHEAD = 6
LAG_REGROUP = 1
LAG_QUANTISE = 1
LAG_MULTIPLY = 4
LAG_SUM = 5
LAG_INVERT = 6
LAG_NORMALISE = 7
LAG_TRANSPOSE_BACK = 9
LAG_STAGE = 9
LAG_HEAD_SUM = 6
LAG_HEAD_SCALE = 7
BY_CHANNEL_EVERY = 3
LAST_BY_CHANNEL = 3
LAST_FRAMES = 2

FLOPS = 2 * TOKENS * CHANNELS * KINDS * HEADS * HEAD_DIM


def frames_of(c):
    return range(c * CHUNK // FRAME, ((c + 1) * CHUNK - 1) // FRAME + 1)


def kinds_of_frame(f):
    return 1 if f % FRAMES_PER_CLIP == 0 else KINDS


def kinds_of(c):
    return max(kinds_of_frame(f) for f in frames_of(c))


def by_channel(c):
    wanted = c % BY_CHANNEL_EVERY == 1 or c < LAST_BY_CHANNEL
    return wanted and all(kinds_of_frame(f) == kinds_of(c) for f in frames_of(c))


def tile_costvolumeattention17_pa_t_kernel(tc, x, q_w, k_w, out_0, out_1):
    nc = tc.nc
    assert TOKENS == CHUNKS * CHUNK

    x_chunks = x.flatten_outer_dims().rearrange("(c r p) k -> c p r k", p=P, r=ROWS)
    q_frames = out_0.rearrange("(b h t) d i j -> b t d h (i j)", b=CLIPS, h=HEADS)
    k_frames = out_1.rearrange("(b h t) d i j -> b t d h (i j)", b=CLIPS, h=HEADS)

    with ExitStack() as ctx:
        ctx.enter_context(tc.manual_schedule())
        keep = ctx.enter_context(tc.tile_pool(name="keep", bufs=1))
        loads = ctx.enter_context(tc.tile_pool(name="loads", bufs=LOADS_AHEAD + 2))
        work = ctx.enter_context(tc.tile_pool(name="work", bufs=4))
        psum_short = ctx.enter_context(tc.psum_pool(name="psum_short", bufs=4))
        psum_mx = ctx.enter_context(tc.psum_pool(name="psum_mx", bufs=4))

        identity = keep.tile([P, P], F32)
        make_identity(nc, identity[:])

        def transpose_words(rows):
            words = rows.bitcast(F32)
            flipped = psum_short.tile([P, ROWS, HALVES, P], F32, name="short")
            for r in range(ROWS):
                for u in range(HALVES):
                    first = (r * HALVES + u) * P
                    nc.tensor.transpose(flipped[:, r, u, :], words[:, first : first + P], identity[:])
            return flipped

        def regroup(flipped):
            grouped = work.tile([P, CHUNK * PACK], BF16, name="grouped", align_bytes=64)
            nc.scalar.copy(
                out=grouped[:].bitcast(F32).rearrange("q (r m u) -> q r m u", r=ROWS, u=HALVES),
                in_=flipped[:].rearrange("q r u m -> q r m u"),
            )
            return grouped

        def regroup_weights(flipped):
            grouped = work.tile([P, CHUNK * PACK], BF16, name="grouped", align_bytes=64)
            for k in range(KINDS):
                nc.scalar.copy(
                    out=grouped[:, k * P * PACK : (k + 1) * P * PACK]
                    .bitcast(F32)
                    .rearrange("q (d h u) -> q d h u", h=HEADS, u=HALVES),
                    in_=flipped[:, k, :, :].rearrange("q u (h d) -> q d h u", h=HEADS),
                )
            return grouped

        def quantise(grouped, codes, scales):
            nc.vector.quantize_mx(out=codes[:].bitcast(FP8X4), scales=scales[:], in_=grouped[:])

        x_rows, x_flipped, x_grouped, x_codes, x_scales = {}, {}, {}, {}, {}
        products, squares, sums, inverse_norms, normalised, out_flipped = {}, {}, {}, {}, {}, {}
        outputs = keep.tile([P, KINDS, TOKENS], F32)
        missing = {f: FRAME for f in range(FRAMES)}

        def load(c):
            x_rows[c] = loads.tile([P, ROWS * CHANNELS], BF16, name="x_rows")
            nc.sync.dma_start(out=x_rows[c][:].rearrange("p (r k) -> p r k", r=ROWS), in_=x_chunks[c])

        def transpose_in(c):
            x_flipped[c] = transpose_words(x_rows[c][:])

        def regroup_chunk(c):
            x_grouped[c] = regroup(x_flipped[c])

        def quantise_chunk(c):
            x_codes[c] = work.tile([P, CHUNK], U32, name="x_codes", align_bytes=64)
            x_scales[c] = work.tile([P, CHUNK], U8, name="x_scales", align_bytes=64)
            quantise(x_grouped[c], x_codes[c], x_scales[c])

        def multiply(c):
            if by_channel(c):
                products[c] = psum_mx.tile([P, KINDS, CHUNK], F32, name="products")
                for k in range(kinds_of(c)):
                    nc.tensor.matmul_mx(
                        out=products[c][:, k, :],
                        lhsT=w_codes[:, k * P : (k + 1) * P].bitcast(FP8X4),
                        lhsT_scale=w_scales[:, k * P : (k + 1) * P],
                        rhs=x_codes[c][:].bitcast(FP8X4),
                        rhs_scale=x_scales[c][:],
                        start=True,
                        stop=True,
                    )
                return
            products[c] = psum_mx.tile([P, ROWS, KINDS, P], F32, name="products")
            width = kinds_of(c) * P
            for r in range(ROWS):
                nc.tensor.matmul_mx(
                    out=products[c][:, r, 0 : kinds_of(c), :].rearrange("p k e -> p (k e)"),
                    lhsT=x_codes[c][:, r * P : (r + 1) * P].bitcast(FP8X4),
                    lhsT_scale=x_scales[c][:, r * P : (r + 1) * P],
                    rhs=w_codes[:, 0:width].bitcast(FP8X4),
                    rhs_scale=w_scales[:, 0:width],
                    start=True,
                    stop=True,
                )

        def square(c):
            if by_channel(c):
                squares[c] = work.tile([P, KINDS, CHUNK], F32, name="squares")
                live = slice(0, kinds_of(c))
                nc.scalar.activation(out=squares[c][:, live], in_=products[c][:, live], func=ACT.Square)
                return
            sets = ROWS * kinds_of(c)
            squares[c] = work.tile([P, ROWS * KINDS, HEADS, HEAD_DIM], F32, name="squares")
            nc.scalar.activation(
                out=squares[c][:, 0:sets],
                in_=products[c][:, :, 0 : kinds_of(c)].rearrange("p r k (d h) -> p (r k) h d", h=HEADS),
                func=ACT.Square,
            )


        def sum_squares(c):
            sets = ROWS * kinds_of(c)
            sums[c] = work.tile([P, ROWS * KINDS, HEADS], F32, name="sums")
            nc.vector.tensor_reduce(
                out=sums[c][:, 0:sets], in_=squares[c][:, 0:sets], axis=mybir.AxisListType.X, op=ALU.add
            )

        def clamp(c):
            live = sums[c][:, 0 : ROWS * kinds_of(c)]
            nc.vector.tensor_scalar_max(out=live, in0=live, scalar1=EPS * EPS)

        def invert(c):
            sets = ROWS * kinds_of(c)
            inverse_norms[c] = work.tile([P, ROWS * KINDS, HEADS], F32, name="inverse_norms")
            nc.scalar.activation(out=inverse_norms[c][:, 0:sets], in_=sums[c][:, 0:sets], func=ACT.Abs_reciprocal_sqrt)

        def normalise(c):
            sets = ROWS * kinds_of(c)
            normalised[c] = work.tile([P, ROWS * KINDS, HEAD_DIM, HEADS], F32, name="normalised")
            nc.vector.tensor_tensor(
                out=normalised[c][:, 0:sets],
                in0=products[c][:, :, 0 : kinds_of(c)].rearrange("p r k (d h) -> p (r k) d h", h=HEADS),
                in1=inverse_norms[c][:, 0:sets].unsqueeze(2).to_broadcast([P, sets, HEAD_DIM, HEADS]),
                op=ALU.mult,
            )

        def transpose_back(c):
            out_flipped[c] = psum_short.tile([P, KINDS, CHUNK], F32, name="short")
            for k in range(kinds_of(c)):
                for r in range(ROWS):
                    nc.tensor.transpose(
                        out_flipped[c][:, k, r * P : (r + 1) * P],
                        normalised[c][:, r * kinds_of(c) + k, :, :].rearrange("p d h -> p (d h)"),
                        identity[:],
                    )

        def stage(c):
            copy = nc.scalar.copy if c % BY_CHANNEL_EVERY == 2 else nc.vector.tensor_copy
            place(c, lambda out, kinds: copy(out=out, in_=out_flipped[c][:, kinds]))


        def sum_heads(c):
            sums[c] = psum_short.tile([P, KINDS, CHUNK], F32, name="short")
            nc.tensor.matmul(
                sums[c][:, 0 : kinds_of(c)].rearrange("e k n -> e (k n)"),
                lhsT=same_head[:],
                rhs=squares[c][:, 0 : kinds_of(c)].rearrange("e k n -> e (k n)"),
                start=True,
                stop=True,
            )

        def invert_heads(c):
            inverse_norms[c] = work.tile([P, KINDS, CHUNK], F32, name="wide_inverse_norms")
            live = slice(0, kinds_of(c))
            nc.scalar.activation(out=inverse_norms[c][:, live], in_=sums[c][:, live], func=ACT.Abs_reciprocal_sqrt)

        def scale_heads(c):
            place(
                c,
                lambda out, kinds: nc.vector.scalar_tensor_tensor(
                    out=out,
                    in0=inverse_norms[c][:, kinds],
                    scalar=1.0 / EPS,
                    in1=products[c][:, kinds],
                    op0=ALU.min,
                    op1=ALU.mult,
                ),
            )


        def place(c, write):
            kinds = slice(0, kinds_of(c))
            write(outputs[:, kinds, c * CHUNK : (c + 1) * CHUNK], kinds)
            for f in frames_of(c):
                missing[f] -= min((c + 1) * CHUNK, (f + 1) * FRAME) - max(c * CHUNK, f * FRAME)
                head = -f * FRAME % CHUNK or CHUNK
                if f < LAST_FRAMES and missing[f] == head:
                    store(f, head, FRAME)
                if missing[f] == 0:
                    store(f, 0, head if f < LAST_FRAMES else FRAME)

        def store(f, first, last):
            b, t = divmod(f, FRAMES_PER_CLIP)
            span = slice(first, last)
            results = outputs[:, :, f * FRAME + first : f * FRAME + last]
            nc.sync.dma_start(out=q_frames[b, t][:, :, span], in_=results[:, 0])
            if t > 0:
                nc.sync.dma_start(out=k_frames[b, t - 1][:, :, span], in_=results[:, 1])
            if t == FRAMES_PER_CLIP - 1:
                nc.sync.dma_start(out=k_frames[b, t][:, :, span], in_=results[:, 1])

        def run(step, turn, which=None):
            c = CHUNKS - 1 - turn
            if 0 <= c < CHUNKS and which in (None, by_channel(c)):
                step(c)

        w_rows = keep.tile([P, KINDS * CHANNELS], BF16)
        nc.sync.dma_start(out=w_rows[:, 0:CHANNELS], in_=q_w)
        nc.sync.dma_start(out=w_rows[:, CHANNELS : KINDS * CHANNELS], in_=k_w)
        for turn in range(LOADS_AHEAD):
            run(load, turn)
        warm = keep.tile([P, 1], F32)
        nc.vector.memset(warm[:], 1.0)
        nc.scalar.activation(out=warm[:], in_=warm[:], func=ACT.Abs_reciprocal_sqrt)
        head_of = keep.tile([P, HEADS], F32)
        same_head = keep.tile([P, P], F32)
        nc.vector.tensor_reduce(
            out=head_of[:], in_=identity[:].rearrange("e (d h) -> e h d", h=HEADS), axis=mybir.AxisListType.X, op=ALU.add
        )
        nc.vector.tensor_copy(
            out=same_head[:].rearrange("e (d h) -> e d h", h=HEADS),
            in_=head_of[:].unsqueeze(1).to_broadcast([P, HEAD_DIM, HEADS]),
        )
        w_codes = keep.tile([P, KINDS * P], U32, align_bytes=64)
        w_scales = keep.tile([P, KINDS * P], U8, align_bytes=64)
        quantise(regroup_weights(transpose_words(w_rows[:])), w_codes, w_scales)

        for n in range(CHUNKS + LAG_STAGE):
            run(load, n + LOADS_AHEAD)
            run(scale_heads, n - LAG_HEAD_SCALE, True)
            run(transpose_back, n - LAG_TRANSPOSE_BACK, False)
            run(regroup_chunk, n - LAG_REGROUP)
            run(sum_heads, n - LAG_HEAD_SUM, True)
            run(multiply, n - LAG_MULTIPLY)
            run(stage, n - LAG_STAGE, False)
            run(invert_heads, n - LAG_HEAD_SUM, True)
            run(normalise, n - LAG_NORMALISE, False)
            run(invert, n - LAG_INVERT, False)
            run(sum_squares, n - LAG_SUM, False)
            run(quantise_chunk, n - LAG_QUANTISE)
            run(transpose_in, n)
            run(square, n - LAG_MULTIPLY)
            run(clamp, n - LAG_SUM, False)
